import numpy as np
import ml_dtypes


def mxq(x, axis, fmt="e4m3"):
    dtype, down = {"e4m3": (ml_dtypes.float8_e4m3fn, 7), "e5m2": (ml_dtypes.float8_e5m2, 14)}[fmt]
    v = np.moveaxis(np.asarray(x, np.float32).astype(ml_dtypes.bfloat16).astype(np.float64), axis, -1)
    blocks = v.reshape(v.shape[:-1] + (-1, 32))
    amax = np.abs(blocks).max(-1, keepdims=True)
    byte = np.maximum(np.where(amax > 0, np.frexp(amax)[1] - 1 + 127, 0) - down, 1)
    scale = np.exp2(byte - 127.0)
    codes = (blocks / scale).astype(np.float32).astype(dtype).astype(np.float64)
    return np.moveaxis((codes * scale).reshape(v.shape), -1, axis)


WIDE = False


def mx_kscale(k):
    if not WIDE:
        return np.ones(k)
    levels = np.array([10, -10, 5, -5, 0])
    a = np.random.permutation(np.resize(levels, k // 512 * 4)).reshape(k // 512, 4)
    idx = np.arange(k)
    return np.exp2(a[idx // 512, idx % 128 // 32])


BF16 = ml_dtypes.bfloat16


def bf(x):
    return np.asarray(x, np.float32).astype(BF16)


def f64(x):
    return np.asarray(x).astype(np.float64)


B, C, D, T, H, W, P = 1, 1024, 512, 8, 16, 16, 2
N = T * H * W
BN_EPS = 1e-5


def setup_inputs():
    s = mx_kscale(D)
    return {"y": bf(np.random.standard_normal((B, D, T, H, W)) * 0.3 * np.sqrt(D) * s[None, :, None, None, None]),
            "w_w": bf(np.random.standard_normal((C, D)) / (0.3 * D) / s[None, :]),
            "w_b": bf(np.random.standard_normal(C) * 0.3),
            "bn_gamma": bf(np.random.standard_normal(C))}


def reference(y, w_w, w_b, bn_gamma):
    wy = (mxq(f64(w_w), 1, "e4m3") @ mxq(f64(y).reshape(B, D, N), 1, "e4m3")) + f64(w_b)[None, :, None]
    wy = wy.reshape(B, C, T, H, W)
    mean = wy.mean(axis=(0, 2, 3, 4))
    var = wy.var(axis=(0, 2, 3, 4))
    return wy, mean, f64(bn_gamma) / np.sqrt(var + BN_EPS)

@@ -1,0 +1,165 @@
+from contextlib import ExitStack
+
+import concourse.mybir as mybir
+from concourse.masks import make_identity
+
+FP8X4 = mybir.dt.float8_e4m3fn_x4
+BF16 = mybir.dt.bfloat16
+F32 = mybir.dt.float32
+U32 = mybir.dt.uint32
+U8 = mybir.dt.uint8
+ACT = mybir.ActivationFunctionType
+
+P = 128
+PACK = 4
+D_IN = P * PACK
+CHANNELS = 1024
+POSITIONS = 2048
+CH_TILES = CHANNELS // P
+CHUNK = 512
+CHUNKS = POSITIONS // CHUNK
+HALF_CHUNKS = 2
+HALVES = CHUNKS // HALF_CHUNKS
+PAIR = 2
+PAIRS = CH_TILES // PAIR
+W_LOADS = 2
+PAIRS_PER_LOAD = PAIRS // W_LOADS
+RUN = 4
+VECTOR_COLS = 384
+BN_STATS_DIM = 6
+BN_EPS = 1e-5
+
+FLOPS = 2 * CHANNELS * D_IN * POSITIONS
+
+
+def tile_nonlocalblocknd_pc_kernel(tc, y, w_w, w_b, bn_gamma, out_0, out_1, out_2):
+    nc = tc.nc
+
+    y_rows = y[0].rearrange("(p j) t h w -> p j (t h w)", j=PACK)
+    w_rows = w_w.rearrange("(p m) d -> p (m d)", m=CH_TILES)
+    wy_rows = out_0[0].rearrange("(p m) t h w -> p m (t h w)", m=CH_TILES)
+
+    with ExitStack() as ctx:
+        consts = ctx.enter_context(tc.tile_pool(name="consts", bufs=1))
+        y_pool = ctx.enter_context(tc.tile_pool(name="y_pool", bufs=CHUNKS))
+        w_raw_pool = ctx.enter_context(tc.tile_pool(name="w_raw_pool", bufs=W_LOADS))
+        w_pool = ctx.enter_context(tc.tile_pool(name="w_pool", bufs=PAIRS))
+        wy_pool = ctx.enter_context(tc.tile_pool(name="wy_pool", bufs=CH_TILES * HALVES))
+        psum_w = ctx.enter_context(tc.psum_pool(name="psum_w", bufs=2))
+        psum_acc = ctx.enter_context(tc.psum_pool(name="psum_acc", bufs=6))
+
+        eps = consts.tile([P, 1], F32)
+        nc.vector.memset(eps[:], BN_EPS)
+        table_warmer = consts.tile([P, 1], F32)
+        nc.scalar.activation(out=table_warmer[:], in_=eps[:], func=ACT.Sqrt)
+        identity = consts.tile([P, P], F32)
+        make_identity(nc, identity[:])
+
+        bias_bf16 = consts.tile([P, CH_TILES], BF16)
+        nc.scalar.dma_start(out=bias_bf16[:], in_=w_b.rearrange("(p m) -> p m", m=CH_TILES))
+        gamma_bf16 = consts.tile([P, CH_TILES], BF16)
+        nc.scalar.dma_start(out=gamma_bf16[:], in_=bn_gamma.rearrange("(p m) -> p m", m=CH_TILES))
+
+        def load_y_chunk(c):
+            y_raw = y_pool.tile([P, PACK, CHUNK], BF16)
+            nc.sync.dma_start(out=y_raw[:], in_=y_rows[:, :, c * CHUNK : (c + 1) * CHUNK])
+            return y_raw
+
+        def load_w_part(part):
+            width = CH_TILES * D_IN // W_LOADS
+            w_raw = w_raw_pool.tile([P, width], BF16)
+            nc.sync.dma_start(out=w_raw[:], in_=w_rows[:, part * width : (part + 1) * width])
+            return w_raw
+
+        y_raws = [load_y_chunk(0)]
+        w_raws = [load_w_part(0)]
+        y_raws.append(load_y_chunk(1))
+        w_raws.append(load_w_part(1))
+        y_raws.append(load_y_chunk(2))
+        y_raws.append(load_y_chunk(3))
+
+        bias = consts.tile([P, CH_TILES], F32)
+        nc.vector.tensor_copy(out=bias[:], in_=bias_bf16[:])
+        gamma = consts.tile([P, CH_TILES], F32)
+        nc.vector.tensor_copy(out=gamma[:], in_=gamma_bf16[:])
+
+        def quantise_y_chunk(y_raw):
+            y_grouped = y_pool.tile([P, CHUNK, PACK], BF16, align_bytes=64)
+            src = y_raw[:].rearrange("p j (c i) -> p c j i", i=RUN)
+            dst = y_grouped[:].rearrange("p (c i) j -> p c j i", i=RUN)
+            split = VECTOR_COLS // RUN
+            nc.vector.tensor_copy(out=dst[:, :split], in_=src[:, :split])
+            nc.scalar.copy(out=dst[:, split:], in_=src[:, split:])
+            y_codes = y_pool.tile([P, CHUNK], U32, align_bytes=64)
+            y_scales = y_pool.tile([P, CHUNK], U8, align_bytes=64)
+            nc.vector.quantize_mx(
+                out=y_codes[:].bitcast(FP8X4),
+                scales=y_scales[:],
+                in_=y_grouped[:].rearrange("p n j -> p (n j)"),
+            )
+            return y_codes, y_scales
+
+        def quantise_w_pair(w_raw, first_tile):
+            words = w_raw[:].bitcast(F32).rearrange("c (m p u) -> c m u p", p=P, u=2)
+            w_t = psum_w.tile([P, PAIR, 2, P], F32)
+            for t in range(PAIR):
+                for u in range(2):
+                    nc.tensor.transpose(w_t[:, t, u, :], words[:, first_tile + t, u, :], identity[:])
+            w_grouped = w_pool.tile([P, PAIR * P * PACK], BF16, align_bytes=64)
+            nc.scalar.copy(
+                out=w_grouped[:].bitcast(F32).rearrange("p (t c u) -> p t c u", t=PAIR, u=2),
+                in_=w_t[:].rearrange("p t u c -> p t c u"),
+            )
+            w_codes = w_pool.tile([P, PAIR * P], U32, align_bytes=64)
+            w_scales = w_pool.tile([P, PAIR * P], U8, align_bytes=64)
+            nc.vector.quantize_mx(out=w_codes[:].bitcast(FP8X4), scales=w_scales[:], in_=w_grouped[:])
+            return w_codes, w_scales
+
+        y_mx = [quantise_y_chunk(y_raws[0])]
+        w_mx = [quantise_w_pair(w_raws[0], 0)]
+        y_mx.append(quantise_y_chunk(y_raws[1]))
+        for pair in range(1, PAIRS):
+            w_mx.append(quantise_w_pair(w_raws[pair // PAIRS_PER_LOAD], (pair % PAIRS_PER_LOAD) * PAIR))
+        y_mx.append(quantise_y_chunk(y_raws[2]))
+        y_mx.append(quantise_y_chunk(y_raws[3]))
+
+        stats = consts.tile([P, CH_TILES, CHUNKS, BN_STATS_DIM], F32)
+        mean_var = consts.tile([P, CH_TILES, 2], F32)
+        for half in range(HALVES):
+            for m in range(CH_TILES):
+                w_codes, w_scales = w_mx[m // PAIR]
+                w_cols = slice((m % PAIR) * P, (m % PAIR + 1) * P)
+                wy = wy_pool.tile([P, HALF_CHUNKS * CHUNK], F32)
+                for b in range(HALF_CHUNKS):
+                    c = half * HALF_CHUNKS + b
+                    y_codes, y_scales = y_mx[c]
+                    acc = psum_acc.tile([P, CHUNK], F32)
+                    nc.tensor.matmul_mx(
+                        out=acc[:],
+                        lhsT=w_codes[:, w_cols].bitcast(FP8X4),
+                        lhsT_scale=w_scales[:, w_cols],
+                        rhs=y_codes[:].bitcast(FP8X4),
+                        rhs_scale=y_scales[:],
+                        start=True,
+                        stop=True,
+                    )
+                    cols = slice(b * CHUNK, (b + 1) * CHUNK)
+                    nc.scalar.activation(
+                        out=wy[:, cols], in_=acc[:], func=ACT.Identity, bias=bias[:, m : m + 1], scale=1.0
+                    )
+                    nc.vector.bn_stats(out=stats[:, m, c, :], in_=wy[:, cols])
+                first = half * HALF_CHUNKS * CHUNK
+                nc.sync.dma_start(out=wy_rows[:, m, first : first + HALF_CHUNKS * CHUNK], in_=wy[:])
+                if half == HALVES - 1:
+                    nc.vector.bn_aggr(out=mean_var[:, m, :], in_=stats[:, m].rearrange("p c s -> p (c s)"))
+
+        std = consts.tile([P, CH_TILES], F32)
+        nc.scalar.activation(out=std[:], in_=mean_var[:, :, 1], func=ACT.Sqrt, bias=eps[:], scale=1.0)
+        mean = consts.tile([P, CH_TILES], F32)
+        nc.vector.tensor_copy(out=mean[:], in_=mean_var[:, :, 0])
+        nc.sync.dma_start(out=out_1.rearrange("(p m) -> p m", m=CH_TILES), in_=mean[:])
+        inv_std = consts.tile([P, CH_TILES], F32)
+        nc.vector.reciprocal(out=inv_std[:], in_=std[:])
+        gain = consts.tile([P, CH_TILES], F32)
+        nc.vector.tensor_mul(out=gain[:], in0=inv_std[:], in1=gamma[:])
+        nc.sync.dma_start(out=out_2.rearrange("(p m) -> p m", m=CH_TILES), in_=gain[:])

@@ -9,6 +9,7 @@ F32 = mybir.dt.float32
 U32 = mybir.dt.uint32
 U8 = mybir.dt.uint8
 ACT = mybir.ActivationFunctionType
+ALU = mybir.AluOpType
 
 P = 128
 PACK = 4
@@ -83,13 +84,23 @@ def tile_nonlocalblocknd_pc_kernel(tc, y, w_w, w_b, bn_gamma, out_0, out_1, out_
         gamma = consts.tile([P, CH_TILES], F32)
         nc.vector.tensor_copy(out=gamma[:], in_=gamma_bf16[:])
 
-        def quantise_y_chunk(y_raw):
+        def quantise_y_chunk(y_raw, urgent):
             y_grouped = y_pool.tile([P, CHUNK, PACK], BF16, align_bytes=64)
-            src = y_raw[:].rearrange("p j (c i) -> p c j i", i=RUN)
-            dst = y_grouped[:].rearrange("p (c i) j -> p c j i", i=RUN)
-            split = VECTOR_COLS // RUN
-            nc.vector.tensor_copy(out=dst[:, :split], in_=src[:, :split])
-            nc.scalar.copy(out=dst[:, split:], in_=src[:, split:])
+            if urgent:
+                src = y_raw[:].rearrange("p j (c i) -> p c j i", i=RUN)
+                dst = y_grouped[:].rearrange("p (c i) j -> p c j i", i=RUN)
+                split = VECTOR_COLS // RUN
+                nc.vector.tensor_copy(out=dst[:, :split], in_=src[:, :split])
+                nc.scalar.copy(out=dst[:, split:], in_=src[:, split:])
+            else:
+                nc.gpsimd.tensor_scalar(
+                    out=y_grouped[:],
+                    in0=y_raw[:].rearrange("p j n -> p n j"),
+                    scalar1=1.0,
+                    scalar2=0.0,
+                    op0=ALU.mult,
+                    op1=ALU.add,
+                )
             y_codes = y_pool.tile([P, CHUNK], U32, align_bytes=64)
             y_scales = y_pool.tile([P, CHUNK], U8, align_bytes=64)
             nc.vector.quantize_mx(
@@ -115,13 +126,13 @@ def tile_nonlocalblocknd_pc_kernel(tc, y, w_w, w_b, bn_gamma, out_0, out_1, out_
             nc.vector.quantize_mx(out=w_codes[:].bitcast(FP8X4), scales=w_scales[:], in_=w_grouped[:])
             return w_codes, w_scales
 
-        y_mx = [quantise_y_chunk(y_raws[0])]
+        y_mx = [quantise_y_chunk(y_raws[0], True)]
         w_mx = [quantise_w_pair(w_raws[0], 0)]
-        y_mx.append(quantise_y_chunk(y_raws[1]))
+        y_mx.append(quantise_y_chunk(y_raws[1], True))
         for pair in range(1, PAIRS):
             w_mx.append(quantise_w_pair(w_raws[pair // PAIRS_PER_LOAD], (pair % PAIRS_PER_LOAD) * PAIR))
-        y_mx.append(quantise_y_chunk(y_raws[2]))
-        y_mx.append(quantise_y_chunk(y_raws[3]))
+        y_mx.append(quantise_y_chunk(y_raws[2], False))
+        y_mx.append(quantise_y_chunk(y_raws[3], False))
 
         stats = consts.tile([P, CH_TILES, CHUNKS, BN_STATS_DIM], F32)
         mean_var = consts.tile([P, CH_TILES, 2], F32)

@@ -9,7 +9,6 @@ F32 = mybir.dt.float32
 U32 = mybir.dt.uint32
 U8 = mybir.dt.uint8
 ACT = mybir.ActivationFunctionType
-ALU = mybir.AluOpType
 
 P = 128
 PACK = 4
@@ -23,14 +22,14 @@ HALF_CHUNKS = 2
 HALVES = CHUNKS // HALF_CHUNKS
 PAIR = 2
 PAIRS = CH_TILES // PAIR
-W_LOADS = 2
-PAIRS_PER_LOAD = PAIRS // W_LOADS
 RUN = 4
 VECTOR_COLS = 384
 BN_STATS_DIM = 6
 BN_EPS = 1e-5
 
 FLOPS = 2 * CHANNELS * D_IN * POSITIONS
+
+assert PAIRS >= HALF_CHUNKS + 1
 
 
 def tile_nonlocalblocknd_pc_kernel(tc, y, w_w, w_b, bn_gamma, out_0, out_1, out_2):
@@ -43,18 +42,11 @@ def tile_nonlocalblocknd_pc_kernel(tc, y, w_w, w_b, bn_gamma, out_0, out_1, out_
     with ExitStack() as ctx:
         consts = ctx.enter_context(tc.tile_pool(name="consts", bufs=1))
         y_pool = ctx.enter_context(tc.tile_pool(name="y_pool", bufs=CHUNKS))
-        w_raw_pool = ctx.enter_context(tc.tile_pool(name="w_raw_pool", bufs=W_LOADS))
         w_pool = ctx.enter_context(tc.tile_pool(name="w_pool", bufs=PAIRS))
-        wy_pool = ctx.enter_context(tc.tile_pool(name="wy_pool", bufs=CH_TILES * HALVES))
+        wy_pool = ctx.enter_context(tc.tile_pool(name="wy_pool", bufs=PAIRS * HALVES))
         psum_w = ctx.enter_context(tc.psum_pool(name="psum_w", bufs=2))
         psum_acc = ctx.enter_context(tc.psum_pool(name="psum_acc", bufs=6))
-
-        eps = consts.tile([P, 1], F32)
-        nc.vector.memset(eps[:], BN_EPS)
-        table_warmer = consts.tile([P, 1], F32)
-        nc.scalar.activation(out=table_warmer[:], in_=eps[:], func=ACT.Sqrt)
-        identity = consts.tile([P, P], F32)
-        make_identity(nc, identity[:])
+        ctx.enter_context(tc.manual_schedule())
 
         bias_bf16 = consts.tile([P, CH_TILES], BF16)
         nc.scalar.dma_start(out=bias_bf16[:], in_=w_b.rearrange("(p m) -> p m", m=CH_TILES))
@@ -66,41 +58,35 @@ def tile_nonlocalblocknd_pc_kernel(tc, y, w_w, w_b, bn_gamma, out_0, out_1, out_
             nc.sync.dma_start(out=y_raw[:], in_=y_rows[:, :, c * CHUNK : (c + 1) * CHUNK])
             return y_raw
 
-        def load_w_part(part):
-            width = CH_TILES * D_IN // W_LOADS
-            w_raw = w_raw_pool.tile([P, width], BF16)
-            nc.sync.dma_start(out=w_raw[:], in_=w_rows[:, part * width : (part + 1) * width])
+        def load_w_pair(pair):
+            width = PAIR * D_IN
+            w_raw = w_pool.tile([P, width], BF16)
+            nc.sync.dma_start(out=w_raw[:], in_=w_rows[:, pair * width : (pair + 1) * width])
             return w_raw
 
         y_raws = [load_y_chunk(0)]
-        w_raws = [load_w_part(0)]
-        y_raws.append(load_y_chunk(1))
-        w_raws.append(load_w_part(1))
-        y_raws.append(load_y_chunk(2))
-        y_raws.append(load_y_chunk(3))
+        w_raws = [load_w_pair(0)]
+        y_raws.extend([load_y_chunk(c) for c in range(1, HALF_CHUNKS)])
+        w_raws.extend([load_w_pair(pair) for pair in range(1, PAIRS)])
+        y_raws.extend([load_y_chunk(c) for c in range(HALF_CHUNKS, CHUNKS)])
 
-        bias = consts.tile([P, CH_TILES], F32)
-        nc.vector.tensor_copy(out=bias[:], in_=bias_bf16[:])
-        gamma = consts.tile([P, CH_TILES], F32)
-        nc.vector.tensor_copy(out=gamma[:], in_=gamma_bf16[:])
+        eps = consts.tile([P, 1], F32)
+        nc.vector.memset(eps[:], BN_EPS)
+        table_warmer = consts.tile([P, 1], F32)
+        nc.scalar.activation(out=table_warmer[:], in_=eps[:], func=ACT.Sqrt)
+        identity = consts.tile([P, P], F32)
+        make_identity(nc, identity[:])
 
-        def quantise_y_chunk(y_raw, urgent):
+        def regroup_y_chunk(c):
             y_grouped = y_pool.tile([P, CHUNK, PACK], BF16, align_bytes=64)
-            if urgent:
-                src = y_raw[:].rearrange("p j (c i) -> p c j i", i=RUN)
-                dst = y_grouped[:].rearrange("p (c i) j -> p c j i", i=RUN)
-                split = VECTOR_COLS // RUN
-                nc.vector.tensor_copy(out=dst[:, :split], in_=src[:, :split])
-                nc.scalar.copy(out=dst[:, split:], in_=src[:, split:])
-            else:
-                nc.gpsimd.tensor_scalar(
-                    out=y_grouped[:],
-                    in0=y_raw[:].rearrange("p j n -> p n j"),
-                    scalar1=1.0,
-                    scalar2=0.0,
-                    op0=ALU.mult,
-                    op1=ALU.add,
-                )
+            src = y_raws[c][:].rearrange("p j (c i) -> p c j i", i=RUN)
+            dst = y_grouped[:].rearrange("p (c i) j -> p c j i", i=RUN)
+            split = VECTOR_COLS // RUN
+            nc.vector.tensor_copy(out=dst[:, :split], in_=src[:, :split])
+            nc.scalar.copy(out=dst[:, split:], in_=src[:, split:])
+            return y_grouped
+
+        def quantise_y_chunk(y_grouped):
             y_codes = y_pool.tile([P, CHUNK], U32, align_bytes=64)
             y_scales = y_pool.tile([P, CHUNK], U8, align_bytes=64)
             nc.vector.quantize_mx(
@@ -110,12 +96,12 @@ def tile_nonlocalblocknd_pc_kernel(tc, y, w_w, w_b, bn_gamma, out_0, out_1, out_
             )
             return y_codes, y_scales
 
-        def quantise_w_pair(w_raw, first_tile):
-            words = w_raw[:].bitcast(F32).rearrange("c (m p u) -> c m u p", p=P, u=2)
+        def quantise_w_pair(pair):
+            words = w_raws[pair][:].bitcast(F32).rearrange("c (t p u) -> c t u p", p=P, u=2)
             w_t = psum_w.tile([P, PAIR, 2, P], F32)
             for t in range(PAIR):
                 for u in range(2):
-                    nc.tensor.transpose(w_t[:, t, u, :], words[:, first_tile + t, u, :], identity[:])
+                    nc.tensor.transpose(w_t[:, t, u, :], words[:, t, u, :], identity[:])
             w_grouped = w_pool.tile([P, PAIR * P * PACK], BF16, align_bytes=64)
             nc.scalar.copy(
                 out=w_grouped[:].bitcast(F32).rearrange("p (t c u) -> p t c u", t=PAIR, u=2),
@@ -126,43 +112,62 @@ def tile_nonlocalblocknd_pc_kernel(tc, y, w_w, w_b, bn_gamma, out_0, out_1, out_
             nc.vector.quantize_mx(out=w_codes[:].bitcast(FP8X4), scales=w_scales[:], in_=w_grouped[:])
             return w_codes, w_scales
 
-        y_mx = [quantise_y_chunk(y_raws[0], True)]
-        w_mx = [quantise_w_pair(w_raws[0], 0)]
-        y_mx.append(quantise_y_chunk(y_raws[1], True))
-        for pair in range(1, PAIRS):
-            w_mx.append(quantise_w_pair(w_raws[pair // PAIRS_PER_LOAD], (pair % PAIRS_PER_LOAD) * PAIR))
-        y_mx.append(quantise_y_chunk(y_raws[2], False))
-        y_mx.append(quantise_y_chunk(y_raws[3], False))
+        y_mx = [quantise_y_chunk(regroup_y_chunk(0))]
+        w_mx = [quantise_w_pair(0)]
+        y_mx.extend([quantise_y_chunk(regroup_y_chunk(c)) for c in range(1, HALF_CHUNKS)])
+        bias = consts.tile([P, CH_TILES], F32)
+        nc.scalar.copy(out=bias[:], in_=bias_bf16[:])
+        gamma = consts.tile([P, CH_TILES], F32)
+        nc.scalar.copy(out=gamma[:], in_=gamma_bf16[:])
 
         stats = consts.tile([P, CH_TILES, CHUNKS, BN_STATS_DIM], F32)
         mean_var = consts.tile([P, CH_TILES, 2], F32)
+
+        def aggregate_pair(pair):
+            for m in range(pair * PAIR, (pair + 1) * PAIR):
+                nc.vector.bn_aggr(out=mean_var[:, m, :], in_=stats[:, m].rearrange("p c s -> p (c s)"))
+
         for half in range(HALVES):
-            for m in range(CH_TILES):
-                w_codes, w_scales = w_mx[m // PAIR]
-                w_cols = slice((m % PAIR) * P, (m % PAIR + 1) * P)
-                wy = wy_pool.tile([P, HALF_CHUNKS * CHUNK], F32)
+            for pair in range(PAIRS):
+                prepares_y = half + 1 < HALVES and 0 <= pair - 1 < HALF_CHUNKS
+                w_codes, w_scales = w_mx[pair]
+                wy = wy_pool.tile([P, PAIR, HALF_CHUNKS * CHUNK], F32)
                 for b in range(HALF_CHUNKS):
                     c = half * HALF_CHUNKS + b
                     y_codes, y_scales = y_mx[c]
-                    acc = psum_acc.tile([P, CHUNK], F32)
-                    nc.tensor.matmul_mx(
-                        out=acc[:],
-                        lhsT=w_codes[:, w_cols].bitcast(FP8X4),
-                        lhsT_scale=w_scales[:, w_cols],
-                        rhs=y_codes[:].bitcast(FP8X4),
-                        rhs_scale=y_scales[:],
-                        start=True,
-                        stop=True,
-                    )
                     cols = slice(b * CHUNK, (b + 1) * CHUNK)
-                    nc.scalar.activation(
-                        out=wy[:, cols], in_=acc[:], func=ACT.Identity, bias=bias[:, m : m + 1], scale=1.0
-                    )
-                    nc.vector.bn_stats(out=stats[:, m, c, :], in_=wy[:, cols])
-                first = half * HALF_CHUNKS * CHUNK
-                nc.sync.dma_start(out=wy_rows[:, m, first : first + HALF_CHUNKS * CHUNK], in_=wy[:])
-                if half == HALVES - 1:
-                    nc.vector.bn_aggr(out=mean_var[:, m, :], in_=stats[:, m].rearrange("p c s -> p (c s)"))
+                    for t in range(PAIR):
+                        m = pair * PAIR + t
+                        w_cols = slice(t * P, (t + 1) * P)
+                        acc = psum_acc.tile([P, CHUNK], F32)
+                        nc.tensor.matmul_mx(
+                            out=acc[:],
+                            lhsT=w_codes[:, w_cols].bitcast(FP8X4),
+                            lhsT_scale=w_scales[:, w_cols],
+                            rhs=y_codes[:].bitcast(FP8X4),
+                            rhs_scale=y_scales[:],
+                            start=True,
+                            stop=True,
+                        )
+                        nc.scalar.activation(
+                            out=wy[:, t, cols], in_=acc[:], func=ACT.Identity, bias=bias[:, m : m + 1], scale=1.0
+                        )
+                        nc.vector.bn_stats(out=stats[:, m, c, :], in_=wy[:, t, cols])
+                        if b == HALF_CHUNKS - 1:
+                            first = half * HALF_CHUNKS * CHUNK
+                            nc.sync.dma_start(
+                                out=wy_rows[:, m, first : first + HALF_CHUNKS * CHUNK], in_=wy[:, t, :]
+                            )
+                    if b == 0:
+                        if half == 0 and pair + 1 < PAIRS:
+                            w_mx.append(quantise_w_pair(pair + 1))
+                        if prepares_y:
+                            y_grouped = regroup_y_chunk((half + 1) * HALF_CHUNKS + pair - 1)
+                        if half == HALVES - 1 and pair >= 1:
+                            aggregate_pair(pair - 1)
+                if prepares_y:
+                    y_mx.append(quantise_y_chunk(y_grouped))
+        aggregate_pair(PAIRS - 1)
 
         std = consts.tile([P, CH_TILES], F32)
         nc.scalar.activation(out=std[:], in_=mean_var[:, :, 1], func=ACT.Sqrt, bias=eps[:], scale=1.0)

@@ -9,6 +9,7 @@ F32 = mybir.dt.float32
 U32 = mybir.dt.uint32
 U8 = mybir.dt.uint8
 ACT = mybir.ActivationFunctionType
+ALU = mybir.AluOpType
 
 P = 128
 PACK = 4
@@ -24,6 +25,7 @@ PAIR = 2
 PAIRS = CH_TILES // PAIR
 RUN = 4
 VECTOR_COLS = 384
+GPSIMD_PIECE = 128
 BN_STATS_DIM = 6
 BN_EPS = 1e-5
 
@@ -86,6 +88,20 @@ def tile_nonlocalblocknd_pc_kernel(tc, y, w_w, w_b, bn_gamma, out_0, out_1, out_
             nc.scalar.copy(out=dst[:, split:], in_=src[:, split:])
             return y_grouped
 
+        def regroup_y_chunk_on_gpsimd(c):
+            y_grouped = y_pool.tile([P, CHUNK, PACK], BF16, align_bytes=64)
+            for first in range(0, CHUNK, GPSIMD_PIECE):
+                cols = slice(first, first + GPSIMD_PIECE)
+                nc.gpsimd.tensor_scalar(
+                    out=y_grouped[:, cols, :],
+                    in0=y_raws[c][:, :, cols].rearrange("p j n -> p n j"),
+                    scalar1=1.0,
+                    scalar2=0.0,
+                    op0=ALU.mult,
+                    op1=ALU.add,
+                )
+            return y_grouped
+
         def quantise_y_chunk(y_grouped):
             y_codes = y_pool.tile([P, CHUNK], U32, align_bytes=64)
             y_scales = y_pool.tile([P, CHUNK], U8, align_bytes=64)
@@ -115,6 +131,7 @@ def tile_nonlocalblocknd_pc_kernel(tc, y, w_w, w_b, bn_gamma, out_0, out_1, out_
         y_mx = [quantise_y_chunk(regroup_y_chunk(0))]
         w_mx = [quantise_w_pair(0)]
         y_mx.extend([quantise_y_chunk(regroup_y_chunk(c)) for c in range(1, HALF_CHUNKS)])
+        y_grouped_late = [regroup_y_chunk_on_gpsimd(c) for c in range(HALF_CHUNKS, CHUNKS)]
         bias = consts.tile([P, CH_TILES], F32)
         nc.scalar.copy(out=bias[:], in_=bias_bf16[:])
         gamma = consts.tile([P, CH_TILES], F32)
@@ -161,12 +178,10 @@ def tile_nonlocalblocknd_pc_kernel(tc, y, w_w, w_b, bn_gamma, out_0, out_1, out_
                     if b == 0:
                         if half == 0 and pair + 1 < PAIRS:
                             w_mx.append(quantise_w_pair(pair + 1))
-                        if prepares_y:
-                            y_grouped = regroup_y_chunk((half + 1) * HALF_CHUNKS + pair - 1)
                         if half == HALVES - 1 and pair >= 1:
                             aggregate_pair(pair - 1)
                 if prepares_y:
-                    y_mx.append(quantise_y_chunk(y_grouped))
+                    y_mx.append(quantise_y_chunk(y_grouped_late[pair - 1]))
         aggregate_pair(PAIRS - 1)
 
         std = consts.tile([P, CH_TILES], F32)

@@ -31,8 +31,6 @@ BN_EPS = 1e-5
 
 FLOPS = 2 * CHANNELS * D_IN * POSITIONS
 
-assert PAIRS >= HALF_CHUNKS + 1
-
 
 def tile_nonlocalblocknd_pc_kernel(tc, y, w_w, w_b, bn_gamma, out_0, out_1, out_2):
     nc = tc.nc
@@ -66,11 +64,16 @@ def tile_nonlocalblocknd_pc_kernel(tc, y, w_w, w_b, bn_gamma, out_0, out_1, out_
             nc.sync.dma_start(out=w_raw[:], in_=w_rows[:, pair * width : (pair + 1) * width])
             return w_raw
 
-        y_raws = [load_y_chunk(0)]
-        w_raws = [load_w_pair(0)]
-        y_raws.extend([load_y_chunk(c) for c in range(1, HALF_CHUNKS)])
-        w_raws.extend([load_w_pair(pair) for pair in range(1, PAIRS)])
-        y_raws.extend([load_y_chunk(c) for c in range(HALF_CHUNKS, CHUNKS)])
+        y_raws = {}
+        w_raws = {}
+        w_raws[0] = load_w_pair(0)
+        w_raws[1] = load_w_pair(1)
+        y_raws[0] = load_y_chunk(0)
+        w_raws[2] = load_w_pair(2)
+        w_raws[3] = load_w_pair(3)
+        y_raws[1] = load_y_chunk(1)
+        y_raws[2] = load_y_chunk(2)
+        y_raws[3] = load_y_chunk(3)
 
         eps = consts.tile([P, 1], F32)
         nc.vector.memset(eps[:], BN_EPS)
@@ -112,7 +115,7 @@ def tile_nonlocalblocknd_pc_kernel(tc, y, w_w, w_b, bn_gamma, out_0, out_1, out_
             )
             return y_codes, y_scales
 
-        def quantise_w_pair(pair):
+        def transpose_w_pair(pair):
             words = w_raws[pair][:].bitcast(F32).rearrange("c (t p u) -> c t u p", p=P, u=2)
             w_t = psum_w.tile([P, PAIR, 2, P], F32)
             for t in range(PAIR):
@@ -123,65 +126,93 @@ def tile_nonlocalblocknd_pc_kernel(tc, y, w_w, w_b, bn_gamma, out_0, out_1, out_
                 out=w_grouped[:].bitcast(F32).rearrange("p (t c u) -> p t c u", t=PAIR, u=2),
                 in_=w_t[:].rearrange("p t u c -> p t c u"),
             )
+            return w_grouped
+
+        def quantise_w_pair(w_grouped):
             w_codes = w_pool.tile([P, PAIR * P], U32, align_bytes=64)
             w_scales = w_pool.tile([P, PAIR * P], U8, align_bytes=64)
             nc.vector.quantize_mx(out=w_codes[:].bitcast(FP8X4), scales=w_scales[:], in_=w_grouped[:])
             return w_codes, w_scales
 
-        y_mx = [quantise_y_chunk(regroup_y_chunk(0))]
-        w_mx = [quantise_w_pair(0)]
-        y_mx.extend([quantise_y_chunk(regroup_y_chunk(c)) for c in range(1, HALF_CHUNKS)])
-        y_grouped_late = [regroup_y_chunk_on_gpsimd(c) for c in range(HALF_CHUNKS, CHUNKS)]
         bias = consts.tile([P, CH_TILES], F32)
-        nc.scalar.copy(out=bias[:], in_=bias_bf16[:])
         gamma = consts.tile([P, CH_TILES], F32)
-        nc.scalar.copy(out=gamma[:], in_=gamma_bf16[:])
 
         stats = consts.tile([P, CH_TILES, CHUNKS, BN_STATS_DIM], F32)
         mean_var = consts.tile([P, CH_TILES, 2], F32)
+        y_mx = {}
+        w_mx = {}
+        wy_tiles = {}
 
         def aggregate_pair(pair):
             for m in range(pair * PAIR, (pair + 1) * PAIR):
                 nc.vector.bn_aggr(out=mean_var[:, m, :], in_=stats[:, m].rearrange("p c s -> p (c s)"))
 
-        for half in range(HALVES):
-            for pair in range(PAIRS):
-                prepares_y = half + 1 < HALVES and 0 <= pair - 1 < HALF_CHUNKS
-                w_codes, w_scales = w_mx[pair]
-                wy = wy_pool.tile([P, PAIR, HALF_CHUNKS * CHUNK], F32)
-                for b in range(HALF_CHUNKS):
-                    c = half * HALF_CHUNKS + b
-                    y_codes, y_scales = y_mx[c]
-                    cols = slice(b * CHUNK, (b + 1) * CHUNK)
-                    for t in range(PAIR):
-                        m = pair * PAIR + t
-                        w_cols = slice(t * P, (t + 1) * P)
-                        acc = psum_acc.tile([P, CHUNK], F32)
-                        nc.tensor.matmul_mx(
-                            out=acc[:],
-                            lhsT=w_codes[:, w_cols].bitcast(FP8X4),
-                            lhsT_scale=w_scales[:, w_cols],
-                            rhs=y_codes[:].bitcast(FP8X4),
-                            rhs_scale=y_scales[:],
-                            start=True,
-                            stop=True,
-                        )
-                        nc.scalar.activation(
-                            out=wy[:, t, cols], in_=acc[:], func=ACT.Identity, bias=bias[:, m : m + 1], scale=1.0
-                        )
-                        nc.vector.bn_stats(out=stats[:, m, c, :], in_=wy[:, t, cols])
-                        if b == HALF_CHUNKS - 1:
-                            first = half * HALF_CHUNKS * CHUNK
-                            nc.sync.dma_start(
-                                out=wy_rows[:, m, first : first + HALF_CHUNKS * CHUNK], in_=wy[:, t, :]
-                            )
-                    if b == 0:
-                        if half == 0 and pair + 1 < PAIRS:
-                            w_mx.append(quantise_w_pair(pair + 1))
-                        if half == HALVES - 1 and pair >= 1:
-                            aggregate_pair(pair - 1)
-                if prepares_y:
-                    y_mx.append(quantise_y_chunk(y_grouped_late[pair - 1]))
+        def multiply(pair, c, store_chunk):
+            half, b = divmod(c, HALF_CHUNKS)
+            completes = (pair, half) in wy_tiles
+            if not completes:
+                wy_new = wy_pool.tile([P, PAIR, HALF_CHUNKS * CHUNK], F32)
+                wy_tiles[(pair, half)] = wy_new
+            wy = wy_tiles[(pair, half)]
+            w_codes, w_scales = w_mx[pair]
+            y_codes, y_scales = y_mx[c]
+            cols = slice(b * CHUNK, (b + 1) * CHUNK)
+            for t in range(PAIR):
+                m = pair * PAIR + t
+                w_cols = slice(t * P, (t + 1) * P)
+                acc = psum_acc.tile([P, CHUNK], F32)
+                nc.tensor.matmul_mx(
+                    out=acc[:],
+                    lhsT=w_codes[:, w_cols].bitcast(FP8X4),
+                    lhsT_scale=w_scales[:, w_cols],
+                    rhs=y_codes[:].bitcast(FP8X4),
+                    rhs_scale=y_scales[:],
+                    start=True,
+                    stop=True,
+                )
+                nc.scalar.activation(
+                    out=wy[:, t, cols], in_=acc[:], func=ACT.Identity, bias=bias[:, m : m + 1], scale=1.0
+                )
+                nc.vector.bn_stats(out=stats[:, m, c, :], in_=wy[:, t, cols])
+                if not store_chunk and completes:
+                    first = half * HALF_CHUNKS * CHUNK
+                    nc.sync.dma_start(out=wy_rows[:, m, first : first + HALF_CHUNKS * CHUNK], in_=wy[:, t, :])
+            if store_chunk:
+                tiles = slice(pair * PAIR, (pair + 1) * PAIR)
+                nc.sync.dma_start(out=wy_rows[:, tiles, c * CHUNK : (c + 1) * CHUNK], in_=wy[:, :, cols])
+
+        w_grouped_0 = transpose_w_pair(0)
+        w_grouped_1 = transpose_w_pair(1)
+        w_mx[0] = quantise_w_pair(w_grouped_0)
+        y_grouped_0 = regroup_y_chunk(0)
+        y_mx[0] = quantise_y_chunk(y_grouped_0)
+        w_mx[1] = quantise_w_pair(w_grouped_1)
+        w_grouped_2 = transpose_w_pair(2)
+        w_mx[2] = quantise_w_pair(w_grouped_2)
+        w_grouped_3 = transpose_w_pair(3)
+        w_mx[3] = quantise_w_pair(w_grouped_3)
+        nc.scalar.copy(out=bias[:], in_=bias_bf16[:])
+        nc.scalar.copy(out=gamma[:], in_=gamma_bf16[:])
+        y_grouped_late = {}
+        for c in range(1, CHUNKS):
+            y_grouped_late[c] = regroup_y_chunk_on_gpsimd(c)
+
+        multiply(0, 0, True)
+        multiply(1, 0, True)
+        y_mx[1] = quantise_y_chunk(y_grouped_late[1])
+        multiply(2, 0, True)
+        multiply(3, 0, True)
+        multiply(0, 1, True)
+        y_mx[2] = quantise_y_chunk(y_grouped_late[2])
+        multiply(1, 1, True)
+        multiply(2, 1, True)
+        y_mx[3] = quantise_y_chunk(y_grouped_late[3])
+        multiply(3, 1, True)
+        for pair in range(PAIRS):
+            multiply(pair, 2, False)
+            if pair >= 1:
+                aggregate_pair(pair - 1)
+            multiply(pair, 3, False)
         aggregate_pair(PAIRS - 1)
 
         std = consts.tile([P, CH_TILES], F32)

@@ -27,6 +27,8 @@ RUN = 4
 VECTOR_COLS = 384
 GPSIMD_PIECE = 128
 BN_STATS_DIM = 6
+TRIPLE = 3
+SCALAR_STATS_FROM = 6
 BN_EPS = 1e-5
 
 FLOPS = 2 * CHANNELS * D_IN * POSITIONS
@@ -77,6 +79,8 @@ def tile_nonlocalblocknd_pc_kernel(tc, y, w_w, w_b, bn_gamma, out_0, out_1, out_
 
         eps = consts.tile([P, 1], F32)
         nc.vector.memset(eps[:], BN_EPS)
+        stats = consts.tile([P, CH_TILES, CHUNKS, BN_STATS_DIM], F32)
+        nc.vector.memset(stats[:], float(CHUNK))
         table_warmer = consts.tile([P, 1], F32)
         nc.scalar.activation(out=table_warmer[:], in_=eps[:], func=ACT.Sqrt)
         identity = consts.tile([P, P], F32)
@@ -137,15 +141,33 @@ def tile_nonlocalblocknd_pc_kernel(tc, y, w_w, w_b, bn_gamma, out_0, out_1, out_
         bias = consts.tile([P, CH_TILES], F32)
         gamma = consts.tile([P, CH_TILES], F32)
 
-        stats = consts.tile([P, CH_TILES, CHUNKS, BN_STATS_DIM], F32)
         mean_var = consts.tile([P, CH_TILES, 2], F32)
+        sums = consts.tile([P, CH_TILES], F32)
+        squares = consts.tile([P, CHUNK], BF16)
         y_mx = {}
         w_mx = {}
         wy_tiles = {}
 
         def aggregate_pair(pair):
             for m in range(pair * PAIR, (pair + 1) * PAIR):
-                nc.vector.bn_aggr(out=mean_var[:, m, :], in_=stats[:, m].rearrange("p c s -> p (c s)"))
+                used = CHUNKS * BN_STATS_DIM - (TRIPLE if m >= SCALAR_STATS_FROM else 0)
+                nc.vector.bn_aggr(out=mean_var[:, m, :], in_=stats[:, m].rearrange("p c s -> p (c s)")[:, :used])
+
+        def scalar_stats(pair):
+            wy = wy_tiles[(pair, HALVES - 1)]
+            for t in range(PAIR):
+                m = pair * PAIR + t
+                if m >= SCALAR_STATS_FROM:
+                    tile_mean = stats[:, m, CHUNKS - 1, 1:2]
+                    nc.scalar.activation(out=tile_mean, in_=sums[:, m : m + 1], func=ACT.Copy, scale=1.0 / CHUNK)
+                    nc.scalar.activation(
+                        out=squares[:],
+                        in_=wy[:, t, (HALF_CHUNKS - 1) * CHUNK :],
+                        func=ACT.Square,
+                        bias=tile_mean,
+                        scale=-1.0,
+                        accum_out=stats[:, m, CHUNKS - 1, 2:3],
+                    )
 
         def multiply(pair, c, store_chunk):
             half, b = divmod(c, HALF_CHUNKS)
@@ -170,10 +192,20 @@ def tile_nonlocalblocknd_pc_kernel(tc, y, w_w, w_b, bn_gamma, out_0, out_1, out_
                     start=True,
                     stop=True,
                 )
-                nc.scalar.activation(
-                    out=wy[:, t, cols], in_=acc[:], func=ACT.Identity, bias=bias[:, m : m + 1], scale=1.0
-                )
-                nc.vector.bn_stats(out=stats[:, m, c, :], in_=wy[:, t, cols])
+                if c == CHUNKS - 1 and m >= SCALAR_STATS_FROM:
+                    nc.scalar.activation(
+                        out=wy[:, t, cols],
+                        in_=acc[:],
+                        func=ACT.Identity,
+                        bias=bias[:, m : m + 1],
+                        scale=1.0,
+                        accum_out=sums[:, m : m + 1],
+                    )
+                else:
+                    nc.scalar.activation(
+                        out=wy[:, t, cols], in_=acc[:], func=ACT.Identity, bias=bias[:, m : m + 1], scale=1.0
+                    )
+                    nc.vector.bn_stats(out=stats[:, m, c, :], in_=wy[:, t, cols])
                 if not store_chunk and completes:
                     first = half * HALF_CHUNKS * CHUNK
                     nc.sync.dma_start(out=wy_rows[:, m, first : first + HALF_CHUNKS * CHUNK], in_=wy[:, t, :])
@@ -213,6 +245,7 @@ def tile_nonlocalblocknd_pc_kernel(tc, y, w_w, w_b, bn_gamma, out_0, out_1, out_
             if pair >= 1:
                 aggregate_pair(pair - 1)
             multiply(pair, 3, False)
+            scalar_stats(pair)
         aggregate_pair(PAIRS - 1)
 
         std = consts.tile([P, CH_TILES], F32)

@@ -28,7 +28,7 @@ VECTOR_COLS = 384
 GPSIMD_PIECE = 128
 BN_STATS_DIM = 6
 TRIPLE = 3
-SCALAR_STATS_FROM = 6
+SCALAR_STATS_FROM = 7
 BN_EPS = 1e-5
 
 FLOPS = 2 * CHANNELS * D_IN * POSITIONS
@@ -82,7 +82,7 @@ def tile_nonlocalblocknd_pc_kernel(tc, y, w_w, w_b, bn_gamma, out_0, out_1, out_
         stats = consts.tile([P, CH_TILES, CHUNKS, BN_STATS_DIM], F32)
         nc.vector.memset(stats[:], float(CHUNK))
         table_warmer = consts.tile([P, 1], F32)
-        nc.scalar.activation(out=table_warmer[:], in_=eps[:], func=ACT.Sqrt)
+        nc.scalar.activation(out=table_warmer[:], in_=eps[:], func=ACT.Abs_reciprocal_sqrt)
         identity = consts.tile([P, P], F32)
         make_identity(nc, identity[:])
 
@@ -138,10 +138,8 @@ def tile_nonlocalblocknd_pc_kernel(tc, y, w_w, w_b, bn_gamma, out_0, out_1, out_
             nc.vector.quantize_mx(out=w_codes[:].bitcast(FP8X4), scales=w_scales[:], in_=w_grouped[:])
             return w_codes, w_scales
 
-        bias = consts.tile([P, CH_TILES], F32)
-        gamma = consts.tile([P, CH_TILES], F32)
 
-        mean_var = consts.tile([P, CH_TILES, 2], F32)
+        mean_var = consts.tile([P, 2, CH_TILES], F32)
         sums = consts.tile([P, CH_TILES], F32)
         squares = consts.tile([P, CHUNK], BF16)
         y_mx = {}
@@ -151,7 +149,7 @@ def tile_nonlocalblocknd_pc_kernel(tc, y, w_w, w_b, bn_gamma, out_0, out_1, out_
         def aggregate_pair(pair):
             for m in range(pair * PAIR, (pair + 1) * PAIR):
                 used = CHUNKS * BN_STATS_DIM - (TRIPLE if m >= SCALAR_STATS_FROM else 0)
-                nc.vector.bn_aggr(out=mean_var[:, m, :], in_=stats[:, m].rearrange("p c s -> p (c s)")[:, :used])
+                nc.vector.bn_aggr(out=mean_var[:, :, m], in_=stats[:, m].rearrange("p c s -> p (c s)")[:, :used])
 
         def scalar_stats(pair):
             wy = wy_tiles[(pair, HALVES - 1)]
@@ -197,13 +195,13 @@ def tile_nonlocalblocknd_pc_kernel(tc, y, w_w, w_b, bn_gamma, out_0, out_1, out_
                         out=wy[:, t, cols],
                         in_=acc[:],
                         func=ACT.Identity,
-                        bias=bias[:, m : m + 1],
+                        bias=bias_bf16[:, m : m + 1],
                         scale=1.0,
                         accum_out=sums[:, m : m + 1],
                     )
                 else:
                     nc.scalar.activation(
-                        out=wy[:, t, cols], in_=acc[:], func=ACT.Identity, bias=bias[:, m : m + 1], scale=1.0
+                        out=wy[:, t, cols], in_=acc[:], func=ACT.Identity, bias=bias_bf16[:, m : m + 1], scale=1.0
                     )
                     nc.vector.bn_stats(out=stats[:, m, c, :], in_=wy[:, t, cols])
                 if not store_chunk and completes:
@@ -223,8 +221,6 @@ def tile_nonlocalblocknd_pc_kernel(tc, y, w_w, w_b, bn_gamma, out_0, out_1, out_
         w_mx[2] = quantise_w_pair(w_grouped_2)
         w_grouped_3 = transpose_w_pair(3)
         w_mx[3] = quantise_w_pair(w_grouped_3)
-        nc.scalar.copy(out=bias[:], in_=bias_bf16[:])
-        nc.scalar.copy(out=gamma[:], in_=gamma_bf16[:])
         y_grouped_late = {}
         for c in range(1, CHUNKS):
             y_grouped_late[c] = regroup_y_chunk_on_gpsimd(c)
@@ -248,13 +244,11 @@ def tile_nonlocalblocknd_pc_kernel(tc, y, w_w, w_b, bn_gamma, out_0, out_1, out_
             scalar_stats(pair)
         aggregate_pair(PAIRS - 1)
 
-        std = consts.tile([P, CH_TILES], F32)
-        nc.scalar.activation(out=std[:], in_=mean_var[:, :, 1], func=ACT.Sqrt, bias=eps[:], scale=1.0)
-        mean = consts.tile([P, CH_TILES], F32)
-        nc.vector.tensor_copy(out=mean[:], in_=mean_var[:, :, 0])
-        nc.sync.dma_start(out=out_1.rearrange("(p m) -> p m", m=CH_TILES), in_=mean[:])
+        nc.sync.dma_start(out=out_1.rearrange("(p m) -> p m", m=CH_TILES), in_=mean_var[:, 0, :])
         inv_std = consts.tile([P, CH_TILES], F32)
-        nc.vector.reciprocal(out=inv_std[:], in_=std[:])
+        nc.scalar.activation(
+            out=inv_std[:], in_=mean_var[:, 1, :], func=ACT.Abs_reciprocal_sqrt, bias=eps[:], scale=1.0
+        )
         gain = consts.tile([P, CH_TILES], F32)
-        nc.vector.tensor_mul(out=gain[:], in0=inv_std[:], in1=gamma[:])
+        nc.vector.tensor_mul(out=gain[:], in0=inv_std[:], in1=gamma_bf16[:])
         nc.sync.dma_start(out=out_2.rearrange("(p m) -> p m", m=CH_TILES), in_=gain[:])

@@ -19,8 +19,6 @@ POSITIONS = 2048
 CH_TILES = CHANNELS // P
 CHUNK = 512
 CHUNKS = POSITIONS // CHUNK
-HALF_CHUNKS = 2
-HALVES = CHUNKS // HALF_CHUNKS
 PAIR = 2
 PAIRS = CH_TILES // PAIR
 RUN = 4
@@ -28,7 +26,7 @@ VECTOR_COLS = 384
 GPSIMD_PIECE = 128
 BN_STATS_DIM = 6
 TRIPLE = 3
-SCALAR_STATS_FROM = 7
+QUANTISE_NEXT_AFTER = (1, 0, 0)
 BN_EPS = 1e-5
 
 FLOPS = 2 * CHANNELS * D_IN * POSITIONS
@@ -45,7 +43,7 @@ def tile_nonlocalblocknd_pc_kernel(tc, y, w_w, w_b, bn_gamma, out_0, out_1, out_
         consts = ctx.enter_context(tc.tile_pool(name="consts", bufs=1))
         y_pool = ctx.enter_context(tc.tile_pool(name="y_pool", bufs=CHUNKS))
         w_pool = ctx.enter_context(tc.tile_pool(name="w_pool", bufs=PAIRS))
-        wy_pool = ctx.enter_context(tc.tile_pool(name="wy_pool", bufs=PAIRS * HALVES))
+        wy_pool = ctx.enter_context(tc.tile_pool(name="wy_pool", bufs=PAIRS * CHUNKS))
         psum_w = ctx.enter_context(tc.psum_pool(name="psum_w", bufs=2))
         psum_acc = ctx.enter_context(tc.psum_pool(name="psum_acc", bufs=6))
         ctx.enter_context(tc.manual_schedule())
@@ -140,43 +138,29 @@ def tile_nonlocalblocknd_pc_kernel(tc, y, w_w, w_b, bn_gamma, out_0, out_1, out_
 
 
         mean_var = consts.tile([P, 2, CH_TILES], F32)
-        sums = consts.tile([P, CH_TILES], F32)
+        last_sum = consts.tile([P, 1], F32)
         squares = consts.tile([P, CHUNK], BF16)
         y_mx = {}
         w_mx = {}
-        wy_tiles = {}
+        last_tile = (CH_TILES - 1, CHUNKS - 1)
 
         def aggregate_pair(pair):
             for m in range(pair * PAIR, (pair + 1) * PAIR):
-                used = CHUNKS * BN_STATS_DIM - (TRIPLE if m >= SCALAR_STATS_FROM else 0)
+                used = CHUNKS * BN_STATS_DIM - (TRIPLE if m == last_tile[0] else 0)
                 nc.vector.bn_aggr(out=mean_var[:, :, m], in_=stats[:, m].rearrange("p c s -> p (c s)")[:, :used])
 
-        def scalar_stats(pair):
-            wy = wy_tiles[(pair, HALVES - 1)]
-            for t in range(PAIR):
-                m = pair * PAIR + t
-                if m >= SCALAR_STATS_FROM:
-                    tile_mean = stats[:, m, CHUNKS - 1, 1:2]
-                    nc.scalar.activation(out=tile_mean, in_=sums[:, m : m + 1], func=ACT.Copy, scale=1.0 / CHUNK)
-                    nc.scalar.activation(
-                        out=squares[:],
-                        in_=wy[:, t, (HALF_CHUNKS - 1) * CHUNK :],
-                        func=ACT.Square,
-                        bias=tile_mean,
-                        scale=-1.0,
-                        accum_out=stats[:, m, CHUNKS - 1, 2:3],
-                    )
+        def scalar_stats(wy_last):
+            m, c = last_tile
+            tile_mean = stats[:, m, c, 1:2]
+            nc.scalar.activation(out=tile_mean, in_=last_sum[:], func=ACT.Copy, scale=1.0 / CHUNK)
+            nc.scalar.activation(
+                out=squares[:], in_=wy_last, func=ACT.Square, bias=tile_mean, scale=-1.0, accum_out=stats[:, m, c, 2:3]
+            )
 
-        def multiply(pair, c, store_chunk):
-            half, b = divmod(c, HALF_CHUNKS)
-            completes = (pair, half) in wy_tiles
-            if not completes:
-                wy_new = wy_pool.tile([P, PAIR, HALF_CHUNKS * CHUNK], F32)
-                wy_tiles[(pair, half)] = wy_new
-            wy = wy_tiles[(pair, half)]
+        def multiply(pair, c):
+            wy = wy_pool.tile([P, PAIR, CHUNK], F32)
             w_codes, w_scales = w_mx[pair]
             y_codes, y_scales = y_mx[c]
-            cols = slice(b * CHUNK, (b + 1) * CHUNK)
             for t in range(PAIR):
                 m = pair * PAIR + t
                 w_cols = slice(t * P, (t + 1) * P)
@@ -190,26 +174,23 @@ def tile_nonlocalblocknd_pc_kernel(tc, y, w_w, w_b, bn_gamma, out_0, out_1, out_
                     start=True,
                     stop=True,
                 )
-                if c == CHUNKS - 1 and m >= SCALAR_STATS_FROM:
+                if (m, c) == last_tile:
                     nc.scalar.activation(
-                        out=wy[:, t, cols],
+                        out=wy[:, t, :],
                         in_=acc[:],
                         func=ACT.Identity,
                         bias=bias_bf16[:, m : m + 1],
                         scale=1.0,
-                        accum_out=sums[:, m : m + 1],
+                        accum_out=last_sum[:],
                     )
                 else:
                     nc.scalar.activation(
-                        out=wy[:, t, cols], in_=acc[:], func=ACT.Identity, bias=bias_bf16[:, m : m + 1], scale=1.0
+                        out=wy[:, t, :], in_=acc[:], func=ACT.Identity, bias=bias_bf16[:, m : m + 1], scale=1.0
                     )
-                    nc.vector.bn_stats(out=stats[:, m, c, :], in_=wy[:, t, cols])
-                if not store_chunk and completes:
-                    first = half * HALF_CHUNKS * CHUNK
-                    nc.sync.dma_start(out=wy_rows[:, m, first : first + HALF_CHUNKS * CHUNK], in_=wy[:, t, :])
-            if store_chunk:
-                tiles = slice(pair * PAIR, (pair + 1) * PAIR)
-                nc.sync.dma_start(out=wy_rows[:, tiles, c * CHUNK : (c + 1) * CHUNK], in_=wy[:, :, cols])
+                    nc.vector.bn_stats(out=stats[:, m, c, :], in_=wy[:, t, :])
+            both = slice(pair * PAIR, (pair + 1) * PAIR)
+            nc.sync.dma_start(out=wy_rows[:, both, c * CHUNK : (c + 1) * CHUNK], in_=wy[:])
+            return wy
 
         w_grouped_0 = transpose_w_pair(0)
         w_grouped_1 = transpose_w_pair(1)
@@ -225,23 +206,14 @@ def tile_nonlocalblocknd_pc_kernel(tc, y, w_w, w_b, bn_gamma, out_0, out_1, out_
         for c in range(1, CHUNKS):
             y_grouped_late[c] = regroup_y_chunk_on_gpsimd(c)
 
-        multiply(0, 0, True)
-        multiply(1, 0, True)
-        y_mx[1] = quantise_y_chunk(y_grouped_late[1])
-        multiply(2, 0, True)
-        multiply(3, 0, True)
-        multiply(0, 1, True)
-        y_mx[2] = quantise_y_chunk(y_grouped_late[2])
-        multiply(1, 1, True)
-        multiply(2, 1, True)
-        y_mx[3] = quantise_y_chunk(y_grouped_late[3])
-        multiply(3, 1, True)
-        for pair in range(PAIRS):
-            multiply(pair, 2, False)
-            if pair >= 1:
-                aggregate_pair(pair - 1)
-            multiply(pair, 3, False)
-            scalar_stats(pair)
+        for c in range(CHUNKS):
+            for pair in range(PAIRS):
+                wy = multiply(pair, c)
+                if c + 1 < CHUNKS and pair == QUANTISE_NEXT_AFTER[c]:
+                    y_mx[c + 1] = quantise_y_chunk(y_grouped_late[c + 1])
+                if c == CHUNKS - 1 and pair >= 1:
+                    aggregate_pair(pair - 1)
+        scalar_stats(wy[:, PAIR - 1, :])
         aggregate_pair(PAIRS - 1)
 
         nc.sync.dma_start(out=out_1.rearrange("(p m) -> p m", m=CH_TILES), in_=mean_var[:, 0, :])

@@ -95,7 +95,13 @@ def tile_nonlocalblocknd_pc_kernel(tc, y, w_w, w_b, bn_gamma, out_0, out_1, out_
 
         def regroup_y_chunk_on_gpsimd(c):
             y_grouped = y_pool.tile([P, CHUNK, PACK], BF16, align_bytes=64)
-            for first in range(0, CHUNK, GPSIMD_PIECE):
+            gpsimd_cols = CHUNK
+            if c == 1:
+                gpsimd_cols = CHUNK - GPSIMD_PIECE
+                src = y_raws[c][:].rearrange("p j (c i) -> p c j i", i=RUN)
+                dst = y_grouped[:].rearrange("p (c i) j -> p c j i", i=RUN)
+                nc.vector.tensor_copy(out=dst[:, gpsimd_cols // RUN :], in_=src[:, gpsimd_cols // RUN :])
+            for first in range(0, gpsimd_cols, GPSIMD_PIECE):
                 cols = slice(first, first + GPSIMD_PIECE)
                 nc.gpsimd.tensor_scalar(
                     out=y_grouped[:, cols, :],
@@ -188,8 +194,11 @@ def tile_nonlocalblocknd_pc_kernel(tc, y, w_w, w_b, bn_gamma, out_0, out_1, out_
                         out=wy[:, t, :], in_=acc[:], func=ACT.Identity, bias=bias_bf16[:, m : m + 1], scale=1.0
                     )
                     nc.vector.bn_stats(out=stats[:, m, c, :], in_=wy[:, t, :])
-            both = slice(pair * PAIR, (pair + 1) * PAIR)
-            nc.sync.dma_start(out=wy_rows[:, both, c * CHUNK : (c + 1) * CHUNK], in_=wy[:])
+                if (pair, c) == (PAIRS - 1, CHUNKS - 1):
+                    nc.sync.dma_start(out=wy_rows[:, m, c * CHUNK : (c + 1) * CHUNK], in_=wy[:, t, :])
+            if (pair, c) != (PAIRS - 1, CHUNKS - 1):
+                both = slice(pair * PAIR, (pair + 1) * PAIR)
+                nc.sync.dma_start(out=wy_rows[:, both, c * CHUNK : (c + 1) * CHUNK], in_=wy[:])
             return wy
 
         w_grouped_0 = transpose_w_pair(0)

@@ -26,7 +26,7 @@ VECTOR_COLS = 384
 GPSIMD_PIECE = 128
 BN_STATS_DIM = 6
 TRIPLE = 3
-QUANTISE_NEXT_AFTER = (1, 0, 0)
+QUANTISE_NEXT_AFTER_TILE = 2
 BN_EPS = 1e-5
 
 FLOPS = 2 * CHANNELS * D_IN * POSITIONS
@@ -43,6 +43,7 @@ def tile_nonlocalblocknd_pc_kernel(tc, y, w_w, w_b, bn_gamma, out_0, out_1, out_
         consts = ctx.enter_context(tc.tile_pool(name="consts", bufs=1))
         y_pool = ctx.enter_context(tc.tile_pool(name="y_pool", bufs=CHUNKS))
         w_pool = ctx.enter_context(tc.tile_pool(name="w_pool", bufs=PAIRS))
+        handoff = ctx.enter_context(tc.tile_pool(name="handoff", bufs=1))
         wy_pool = ctx.enter_context(tc.tile_pool(name="wy_pool", bufs=PAIRS * CHUNKS))
         psum_w = ctx.enter_context(tc.psum_pool(name="psum_w", bufs=2))
         psum_acc = ctx.enter_context(tc.psum_pool(name="psum_acc", bufs=6))
@@ -94,7 +95,7 @@ def tile_nonlocalblocknd_pc_kernel(tc, y, w_w, w_b, bn_gamma, out_0, out_1, out_
             return y_grouped
 
         def regroup_y_chunk_on_gpsimd(c):
-            y_grouped = y_pool.tile([P, CHUNK, PACK], BF16, align_bytes=64)
+            y_grouped = handoff.tile([P, CHUNK, PACK], BF16, align_bytes=64)
             gpsimd_cols = CHUNK
             if c == 1:
                 gpsimd_cols = CHUNK - GPSIMD_PIECE
@@ -163,43 +164,35 @@ def tile_nonlocalblocknd_pc_kernel(tc, y, w_w, w_b, bn_gamma, out_0, out_1, out_
                 out=squares[:], in_=wy_last, func=ACT.Square, bias=tile_mean, scale=-1.0, accum_out=stats[:, m, c, 2:3]
             )
 
-        def multiply(pair, c):
-            wy = wy_pool.tile([P, PAIR, CHUNK], F32)
+        def multiply(m, c, wy):
+            pair, t = divmod(m, PAIR)
             w_codes, w_scales = w_mx[pair]
             y_codes, y_scales = y_mx[c]
-            for t in range(PAIR):
-                m = pair * PAIR + t
-                w_cols = slice(t * P, (t + 1) * P)
-                acc = psum_acc.tile([P, CHUNK], F32)
-                nc.tensor.matmul_mx(
-                    out=acc[:],
-                    lhsT=w_codes[:, w_cols].bitcast(FP8X4),
-                    lhsT_scale=w_scales[:, w_cols],
-                    rhs=y_codes[:].bitcast(FP8X4),
-                    rhs_scale=y_scales[:],
-                    start=True,
-                    stop=True,
+            w_cols = slice(t * P, (t + 1) * P)
+            acc = psum_acc.tile([P, CHUNK], F32)
+            nc.tensor.matmul_mx(
+                out=acc[:],
+                lhsT=w_codes[:, w_cols].bitcast(FP8X4),
+                lhsT_scale=w_scales[:, w_cols],
+                rhs=y_codes[:].bitcast(FP8X4),
+                rhs_scale=y_scales[:],
+                start=True,
+                stop=True,
+            )
+            if (m, c) == last_tile:
+                nc.scalar.activation(
+                    out=wy[:, t, :],
+                    in_=acc[:],
+                    func=ACT.Identity,
+                    bias=bias_bf16[:, m : m + 1],
+                    scale=1.0,
+                    accum_out=last_sum[:],
                 )
-                if (m, c) == last_tile:
-                    nc.scalar.activation(
-                        out=wy[:, t, :],
-                        in_=acc[:],
-                        func=ACT.Identity,
-                        bias=bias_bf16[:, m : m + 1],
-                        scale=1.0,
-                        accum_out=last_sum[:],
-                    )
-                else:
-                    nc.scalar.activation(
-                        out=wy[:, t, :], in_=acc[:], func=ACT.Identity, bias=bias_bf16[:, m : m + 1], scale=1.0
-                    )
-                    nc.vector.bn_stats(out=stats[:, m, c, :], in_=wy[:, t, :])
-                if (pair, c) == (PAIRS - 1, CHUNKS - 1):
-                    nc.sync.dma_start(out=wy_rows[:, m, c * CHUNK : (c + 1) * CHUNK], in_=wy[:, t, :])
-            if (pair, c) != (PAIRS - 1, CHUNKS - 1):
-                both = slice(pair * PAIR, (pair + 1) * PAIR)
-                nc.sync.dma_start(out=wy_rows[:, both, c * CHUNK : (c + 1) * CHUNK], in_=wy[:])
-            return wy
+            else:
+                nc.scalar.activation(
+                    out=wy[:, t, :], in_=acc[:], func=ACT.Identity, bias=bias_bf16[:, m : m + 1], scale=1.0
+                )
+                nc.vector.bn_stats(out=stats[:, m, c, :], in_=wy[:, t, :])
 
         w_grouped_0 = transpose_w_pair(0)
         w_grouped_1 = transpose_w_pair(1)
@@ -211,16 +204,24 @@ def tile_nonlocalblocknd_pc_kernel(tc, y, w_w, w_b, bn_gamma, out_0, out_1, out_
         w_mx[2] = quantise_w_pair(w_grouped_2)
         w_grouped_3 = transpose_w_pair(3)
         w_mx[3] = quantise_w_pair(w_grouped_3)
-        y_grouped_late = {}
-        for c in range(1, CHUNKS):
-            y_grouped_late[c] = regroup_y_chunk_on_gpsimd(c)
+        y_grouped_next = regroup_y_chunk_on_gpsimd(1)
 
         for c in range(CHUNKS):
-            for pair in range(PAIRS):
-                wy = multiply(pair, c)
-                if c + 1 < CHUNKS and pair == QUANTISE_NEXT_AFTER[c]:
-                    y_mx[c + 1] = quantise_y_chunk(y_grouped_late[c + 1])
-                if c == CHUNKS - 1 and pair >= 1:
+            positions = slice(c * CHUNK, (c + 1) * CHUNK)
+            for m in range(CH_TILES):
+                pair, t = divmod(m, PAIR)
+                if t == 0:
+                    wy = wy_pool.tile([P, PAIR, CHUNK], F32)
+                multiply(m, c, wy)
+                if (pair, c) == (PAIRS - 1, CHUNKS - 1):
+                    nc.sync.dma_start(out=wy_rows[:, m, positions], in_=wy[:, t, :])
+                elif t == PAIR - 1:
+                    nc.sync.dma_start(out=wy_rows[:, m - t : m + 1, positions], in_=wy[:])
+                if m == QUANTISE_NEXT_AFTER_TILE and c + 1 < CHUNKS:
+                    y_mx[c + 1] = quantise_y_chunk(y_grouped_next)
+                    if c + 2 < CHUNKS:
+                        y_grouped_next = regroup_y_chunk_on_gpsimd(c + 2)
+                if c == CHUNKS - 1 and t == PAIR - 1 and pair >= 1:
                     aggregate_pair(pair - 1)
         scalar_stats(wy[:, PAIR - 1, :])
         aggregate_pair(PAIRS - 1)

from contextlib import ExitStack

import concourse.mybir as mybir
from concourse.masks import make_identity

FP8X4 = mybir.dt.float8_e4m3fn_x4
BF16 = mybir.dt.bfloat16
F32 = mybir.dt.float32
U32 = mybir.dt.uint32
U8 = mybir.dt.uint8
ACT = mybir.ActivationFunctionType
ALU = mybir.AluOpType

P = 128
PACK = 4
D_IN = P * PACK
CHANNELS = 1024
POSITIONS = 2048
CH_TILES = CHANNELS // P
CHUNK = 512
CHUNKS = POSITIONS // CHUNK
PAIR = 2
PAIRS = CH_TILES // PAIR
RUN = 4
VECTOR_COLS = 384
GPSIMD_PIECE = 128
BN_STATS_DIM = 6
TRIPLE = 3
QUANTISE_NEXT_AFTER_TILE = 2
BN_EPS = 1e-5

FLOPS = 2 * CHANNELS * D_IN * POSITIONS


def tile_nonlocalblocknd_pc_kernel(tc, y, w_w, w_b, bn_gamma, out_0, out_1, out_2):
    nc = tc.nc

    y_rows = y[0].rearrange("(p j) t h w -> p j (t h w)", j=PACK)
    w_rows = w_w.rearrange("(p m) d -> p (m d)", m=CH_TILES)
    wy_rows = out_0[0].rearrange("(p m) t h w -> p m (t h w)", m=CH_TILES)

    with ExitStack() as ctx:
        consts = ctx.enter_context(tc.tile_pool(name="consts", bufs=1))
        y_pool = ctx.enter_context(tc.tile_pool(name="y_pool", bufs=CHUNKS))
        w_pool = ctx.enter_context(tc.tile_pool(name="w_pool", bufs=PAIRS))
        handoff = ctx.enter_context(tc.tile_pool(name="handoff", bufs=1))
        wy_pool = ctx.enter_context(tc.tile_pool(name="wy_pool", bufs=PAIRS * CHUNKS))
        psum_w = ctx.enter_context(tc.psum_pool(name="psum_w", bufs=2))
        psum_acc = ctx.enter_context(tc.psum_pool(name="psum_acc", bufs=6))
        ctx.enter_context(tc.manual_schedule())

        bias_bf16 = consts.tile([P, CH_TILES], BF16)
        nc.scalar.dma_start(out=bias_bf16[:], in_=w_b.rearrange("(p m) -> p m", m=CH_TILES))
        gamma_bf16 = consts.tile([P, CH_TILES], BF16)
        nc.scalar.dma_start(out=gamma_bf16[:], in_=bn_gamma.rearrange("(p m) -> p m", m=CH_TILES))

        def load_y_chunk(c):
            y_raw = y_pool.tile([P, PACK, CHUNK], BF16)
            nc.sync.dma_start(out=y_raw[:], in_=y_rows[:, :, c * CHUNK : (c + 1) * CHUNK])
            return y_raw

        def load_w_pair(pair):
            width = PAIR * D_IN
            w_raw = w_pool.tile([P, width], BF16)
            nc.sync.dma_start(out=w_raw[:], in_=w_rows[:, pair * width : (pair + 1) * width])
            return w_raw

        y_raws = {}
        w_raws = {}
        w_raws[0] = load_w_pair(0)
        w_raws[1] = load_w_pair(1)
        y_raws[0] = load_y_chunk(0)
        w_raws[2] = load_w_pair(2)
        w_raws[3] = load_w_pair(3)
        y_raws[1] = load_y_chunk(1)
        y_raws[2] = load_y_chunk(2)
        y_raws[3] = load_y_chunk(3)

        eps = consts.tile([P, 1], F32)
        nc.vector.memset(eps[:], BN_EPS)
        stats = consts.tile([P, CH_TILES, CHUNKS, BN_STATS_DIM], F32)
        nc.vector.memset(stats[:], float(CHUNK))
        table_warmer = consts.tile([P, 1], F32)
        nc.scalar.activation(out=table_warmer[:], in_=eps[:], func=ACT.Abs_reciprocal_sqrt)
        identity = consts.tile([P, P], F32)
        make_identity(nc, identity[:])

        def regroup_y_chunk(c):
            y_grouped = y_pool.tile([P, CHUNK, PACK], BF16, align_bytes=64)
            src = y_raws[c][:].rearrange("p j (c i) -> p c j i", i=RUN)
            dst = y_grouped[:].rearrange("p (c i) j -> p c j i", i=RUN)
            split = VECTOR_COLS // RUN
            nc.vector.tensor_copy(out=dst[:, :split], in_=src[:, :split])
            nc.scalar.copy(out=dst[:, split:], in_=src[:, split:])
            return y_grouped

        def regroup_y_chunk_on_gpsimd(c):
            y_grouped = handoff.tile([P, CHUNK, PACK], BF16, align_bytes=64)
            gpsimd_cols = CHUNK
            if c == 1:
                gpsimd_cols = CHUNK - GPSIMD_PIECE
                src = y_raws[c][:].rearrange("p j (c i) -> p c j i", i=RUN)
                dst = y_grouped[:].rearrange("p (c i) j -> p c j i", i=RUN)
                nc.vector.tensor_copy(out=dst[:, gpsimd_cols // RUN :], in_=src[:, gpsimd_cols // RUN :])
            for first in range(0, gpsimd_cols, GPSIMD_PIECE):
                cols = slice(first, first + GPSIMD_PIECE)
                nc.gpsimd.tensor_scalar(
                    out=y_grouped[:, cols, :],
                    in0=y_raws[c][:, :, cols].rearrange("p j n -> p n j"),
                    scalar1=1.0,
                    scalar2=0.0,
                    op0=ALU.mult,
                    op1=ALU.add,
                )
            return y_grouped

        def quantise_y_chunk(y_grouped):
            y_codes = y_pool.tile([P, CHUNK], U32, align_bytes=64)
            y_scales = y_pool.tile([P, CHUNK], U8, align_bytes=64)
            nc.vector.quantize_mx(
                out=y_codes[:].bitcast(FP8X4),
                scales=y_scales[:],
                in_=y_grouped[:].rearrange("p n j -> p (n j)"),
            )
            return y_codes, y_scales

        def transpose_w_pair(pair):
            words = w_raws[pair][:].bitcast(F32).rearrange("c (t p u) -> c t u p", p=P, u=2)
            w_t = psum_w.tile([P, PAIR, 2, P], F32)
            for t in range(PAIR):
                for u in range(2):
                    nc.tensor.transpose(w_t[:, t, u, :], words[:, t, u, :], identity[:])
            w_grouped = w_pool.tile([P, PAIR * P * PACK], BF16, align_bytes=64)
            nc.scalar.copy(
                out=w_grouped[:].bitcast(F32).rearrange("p (t c u) -> p t c u", t=PAIR, u=2),
                in_=w_t[:].rearrange("p t u c -> p t c u"),
            )
            return w_grouped

        def quantise_w_pair(w_grouped):
            w_codes = w_pool.tile([P, PAIR * P], U32, align_bytes=64)
            w_scales = w_pool.tile([P, PAIR * P], U8, align_bytes=64)
            nc.vector.quantize_mx(out=w_codes[:].bitcast(FP8X4), scales=w_scales[:], in_=w_grouped[:])
            return w_codes, w_scales


        mean_var = consts.tile([P, 2, CH_TILES], F32)
        last_sum = consts.tile([P, 1], F32)
        squares = consts.tile([P, CHUNK], BF16)
        y_mx = {}
        w_mx = {}
        last_tile = (CH_TILES - 1, CHUNKS - 1)

        def aggregate_pair(pair):
            for m in range(pair * PAIR, (pair + 1) * PAIR):
                used = CHUNKS * BN_STATS_DIM - (TRIPLE if m == last_tile[0] else 0)
                nc.vector.bn_aggr(out=mean_var[:, :, m], in_=stats[:, m].rearrange("p c s -> p (c s)")[:, :used])

        def scalar_stats(wy_last):
            m, c = last_tile
            tile_mean = stats[:, m, c, 1:2]
            nc.scalar.activation(out=tile_mean, in_=last_sum[:], func=ACT.Copy, scale=1.0 / CHUNK)
            nc.scalar.activation(
                out=squares[:], in_=wy_last, func=ACT.Square, bias=tile_mean, scale=-1.0, accum_out=stats[:, m, c, 2:3]
            )

        def multiply(m, c, wy):
            pair, t = divmod(m, PAIR)
            w_codes, w_scales = w_mx[pair]
            y_codes, y_scales = y_mx[c]
            w_cols = slice(t * P, (t + 1) * P)
            acc = psum_acc.tile([P, CHUNK], F32)
            nc.tensor.matmul_mx(
                out=acc[:],
                lhsT=w_codes[:, w_cols].bitcast(FP8X4),
                lhsT_scale=w_scales[:, w_cols],
                rhs=y_codes[:].bitcast(FP8X4),
                rhs_scale=y_scales[:],
                start=True,
                stop=True,
            )
            if (m, c) == last_tile:
                nc.scalar.activation(
                    out=wy[:, t, :],
                    in_=acc[:],
                    func=ACT.Identity,
                    bias=bias_bf16[:, m : m + 1],
                    scale=1.0,
                    accum_out=last_sum[:],
                )
            else:
                nc.scalar.activation(
                    out=wy[:, t, :], in_=acc[:], func=ACT.Identity, bias=bias_bf16[:, m : m + 1], scale=1.0
                )
                nc.vector.bn_stats(out=stats[:, m, c, :], in_=wy[:, t, :])

        w_grouped_0 = transpose_w_pair(0)
        w_grouped_1 = transpose_w_pair(1)
        w_mx[0] = quantise_w_pair(w_grouped_0)
        y_grouped_0 = regroup_y_chunk(0)
        y_mx[0] = quantise_y_chunk(y_grouped_0)
        w_mx[1] = quantise_w_pair(w_grouped_1)
        w_grouped_2 = transpose_w_pair(2)
        w_mx[2] = quantise_w_pair(w_grouped_2)
        w_grouped_3 = transpose_w_pair(3)
        w_mx[3] = quantise_w_pair(w_grouped_3)
        y_grouped_next = regroup_y_chunk_on_gpsimd(1)

        for c in range(CHUNKS):
            positions = slice(c * CHUNK, (c + 1) * CHUNK)
            for m in range(CH_TILES):
                pair, t = divmod(m, PAIR)
                if t == 0:
                    wy = wy_pool.tile([P, PAIR, CHUNK], F32)
                multiply(m, c, wy)
                if (pair, c) == (PAIRS - 1, CHUNKS - 1):
                    nc.sync.dma_start(out=wy_rows[:, m, positions], in_=wy[:, t, :])
                elif t == PAIR - 1:
                    nc.sync.dma_start(out=wy_rows[:, m - t : m + 1, positions], in_=wy[:])
                if m == QUANTISE_NEXT_AFTER_TILE and c + 1 < CHUNKS:
                    y_mx[c + 1] = quantise_y_chunk(y_grouped_next)
                    if c + 2 < CHUNKS:
                        y_grouped_next = regroup_y_chunk_on_gpsimd(c + 2)
                if c == CHUNKS - 1 and t == PAIR - 1 and pair >= 1:
                    aggregate_pair(pair - 1)
        scalar_stats(wy[:, PAIR - 1, :])
        aggregate_pair(PAIRS - 1)

        nc.sync.dma_start(out=out_1.rearrange("(p m) -> p m", m=CH_TILES), in_=mean_var[:, 0, :])
        inv_std = consts.tile([P, CH_TILES], F32)
        nc.scalar.activation(
            out=inv_std[:], in_=mean_var[:, 1, :], func=ACT.Abs_reciprocal_sqrt, bias=eps[:], scale=1.0
        )
        gain = consts.tile([P, CH_TILES], F32)
        nc.vector.tensor_mul(out=gain[:], in0=inv_std[:], in1=gamma_bf16[:])
        nc.sync.dma_start(out=out_2.rearrange("(p m) -> p m", m=CH_TILES), in_=gain[:])
